import numpy as np
import ml_dtypes


def mxq(x, axis, fmt="e4m3"):
    dtype, down = {"e4m3": (ml_dtypes.float8_e4m3fn, 7), "e5m2": (ml_dtypes.float8_e5m2, 14)}[fmt]
    v = np.moveaxis(np.asarray(x, np.float32).astype(ml_dtypes.bfloat16).astype(np.float64), axis, -1)
    blocks = v.reshape(v.shape[:-1] + (-1, 32))
    amax = np.abs(blocks).max(-1, keepdims=True)
    byte = np.maximum(np.where(amax > 0, np.frexp(amax)[1] - 1 + 127, 0) - down, 1)
    scale = np.exp2(byte - 127.0)
    codes = (blocks / scale).astype(np.float32).astype(dtype).astype(np.float64)
    return np.moveaxis((codes * scale).reshape(v.shape), -1, axis)


WIDE = False


def mx_kscale(k):
    if not WIDE:
        return np.ones(k)
    levels = np.array([10, -10, 5, -5, 0])
    if k % 512:
        return np.exp2(np.random.permutation(np.resize(levels, k // 32))).repeat(32)
    a = np.empty((k // 512, 16))
    for p in range(k // 512):
        a[p, :8] = np.random.permutation(np.resize(levels, 8))
        for g in range(8):
            far = levels[np.abs(levels - a[p, g]) >= 10]
            a[p, g + 8] = far[np.random.randint(len(far))]
    return np.exp2(a.ravel()).repeat(32)


BF16 = ml_dtypes.bfloat16


def bf(x):
    return np.asarray(x, np.float32).astype(BF16)


def f64(x):
    return np.asarray(x).astype(np.float64)


B, S, IN, OUT = 4, 128, 2048, 2048


def setup_inputs():
    s = mx_kscale(IN)
    w = np.random.standard_normal((OUT, IN + 1))
    w[:, :IN] *= 0.25 / np.sqrt(IN) / s
    w[:, IN] *= 0.5
    return {"x": bf(np.random.standard_normal((B, S, IN)) * s), "weight": bf(w)}


def core(x, weight):
    w = f64(weight)
    in_features = w.shape[1] - 1
    xf = f64(x).reshape(-1, in_features)
    wm, wb = w[:, :in_features], w[:, in_features]
    xq = mxq(xf, 1, "e4m3")
    wq = mxq(wm, 1, "e4m3")
    lin = (xq @ wq.T) + wb
    ab = (np.abs(xq) @ np.abs(wq).T) + np.abs(wb)
    return 0.5 * (lin + ab)


def e4m3fn_bytes(y):
    return np.clip(np.asarray(y, np.float64), -448.0, 448.0).astype(np.float32).astype(ml_dtypes.float8_e4m3fn).view(np.uint8)


def reference(x, weight):
    out = core(x, weight)
    s = np.max(np.abs(out)) / 448.0
    return out, e4m3fn_bytes(out / s)

@@ -1,0 +1,295 @@
+from contextlib import ExitStack
+
+import concourse.mybir as mybir
+from concourse.masks import make_identity
+
+F32 = mybir.dt.float32
+BF16 = mybir.dt.bfloat16
+I32 = mybir.dt.int32
+U8 = mybir.dt.uint8
+FP8X4 = mybir.dt.float8_e4m3fn_x4
+FP8 = mybir.dt.float8_e4m3fn
+ALU = mybir.AluOpType
+ACT = mybir.ActivationFunctionType
+AX = mybir.AxisListType
+
+P = 128
+K = 2048
+TOK = 512
+OUT = 2048
+PASSES = 4
+STEP_COLS = 256
+STEPS = OUT // STEP_COLS
+
+FLOPS = 2 * 2 * TOK * K * OUT
+
+
+def tile_skanlinear_kernel(tc, x, weight, out_0, out_1):
+    nc = tc.nc
+    x2 = x.flatten_outer_dims()
+
+    with ExitStack() as ctx:
+        const = ctx.enter_context(tc.tile_pool(name="const", bufs=1))
+        rawp = ctx.enter_context(tc.tile_pool(name="rawp", bufs=1))
+        qpool = ctx.enter_context(tc.tile_pool(name="qpool", bufs=8))
+        cpool = ctx.enter_context(tc.tile_pool(name="cpool", bufs=3))
+        tpsum = ctx.enter_context(tc.psum_pool(name="tpsum", bufs=4))
+        apsum = ctx.enter_context(tc.psum_pool(name="apsum", bufs=4))
+        ctx.enter_context(tc.manual_schedule())
+
+        x_raw = {}
+        w_raw = {}
+
+        def load_x(b):
+            t = rawp.tile([P, K], BF16, name="xraw%d" % b)
+            nc.sync.dma_start(out=t[:], in_=x2[b * P : (b + 1) * P, :])
+            x_raw[b] = t
+
+        def load_w(i):
+            t = rawp.tile([P, K + 2], BF16, name="wraw%d" % i)
+            nc.sync.dma_start(out=t[:, 0 : K + 1], in_=weight[i * P : (i + 1) * P, :])
+            w_raw[i] = t
+
+        load_x(0)
+        load_x(1)
+        load_w(0)
+        load_w(1)
+        load_x(2)
+        load_x(3)
+        for i in range(2, 16):
+            load_w(i)
+
+        ident = const.tile([P, P], F32, name="ident")
+        make_identity(nc, ident[:])
+        ident_bf = const.tile([P, P], BF16, name="ident_bf")
+        make_identity(nc, ident_bf[:])
+        zeros = const.tile([P, 1], F32, name="zeros")
+        nc.vector.memset(zeros[:], 0.0)
+        warm = const.tile([P, 1], F32, name="warm")
+        nc.scalar.activation(out=warm[:], in_=zeros[:], func=ACT.Abs)
+
+        xc = const.tile([P, 2, PASSES, 2, STEP_COLS], I32, name="xc", align_bytes=64)
+        xs = const.tile([P, 2, PASSES, 2, STEP_COLS], U8, name="xs", align_bytes=64)
+        bias = const.tile([P, OUT], F32, name="bias")
+        stats = const.tile([P, 4 * STEPS], F32, name="stats")
+        o0 = []
+        for m in range(4):
+            t = const.tile([P, OUT], F32, name="o0_%d" % m)
+            o0.append(t)
+
+        banks = {}
+        qtiles = {}
+        codes = {}
+        scales = {}
+        bias_bank = {}
+        accs = {}
+
+        def raw_pair(u):
+            if u[0] == "x":
+                return [x_raw[2 * u[1]], x_raw[2 * u[1] + 1]]
+            return [w_raw[2 * u[1]], w_raw[2 * u[1] + 1]]
+
+        def transposes(u, by_tile, pool):
+            for g in range(PASSES):
+                if pool == "t":
+                    bank = tpsum.tile([P, 2, 2, P], F32, tag="t")
+                else:
+                    bank = apsum.tile([P, 2, 2, P], F32, tag="acc")
+                banks[(u, g)] = bank
+            order = [(g, j) for g in range(PASSES) for j in range(2)]
+            if by_tile:
+                order = [(g, j) for j in range(2) for g in range(PASSES)]
+            pair = raw_pair(u)
+            for g, j in order:
+                words = pair[j][:, 0:K].bitcast(F32)
+                for h in range(2):
+                    nc.tensor.transpose(banks[(u, g)][:, j, h, :], words[:, 256 * g + h : 256 * (g + 1) : 2], ident[:])
+            if u[0] == "x":
+                codes[u] = xc[:, u[1], :, :, :]
+                scales[u] = xs[:, u[1], :, :, :]
+            else:
+                wc = cpool.tile([P, PASSES, 2, STEP_COLS], I32, tag="wc", align_bytes=64)
+                ws = cpool.tile([P, PASSES, 2, STEP_COLS], U8, tag="ws", align_bytes=64)
+                codes[u] = wc[:]
+                scales[u] = ws[:]
+
+        def copy_out(u, g, eng):
+            q = qpool.tile([P, 2, 4 * STEP_COLS], BF16, tag="q", align_bytes=64)
+            qtiles[(u, g)] = q
+            dst = q[:, 0, :].bitcast(F32).rearrange("p (j r h) -> p j r h", j=2, h=2)
+            src = banks[(u, g)][:].rearrange("p j h r -> p j r h")
+            if eng == "v":
+                nc.vector.tensor_copy(out=dst, in_=src)
+            else:
+                nc.scalar.copy(out=dst, in_=src)
+
+        def absolute(u, g, eng):
+            q = qtiles[(u, g)]
+            if eng == "v":
+                nc.vector.tensor_scalar(
+                    out=q[:, 1, :].bitcast(I32),
+                    in0=q[:, 0, :].bitcast(I32),
+                    scalar1=0x7FFF7FFF,
+                    scalar2=None,
+                    op0=ALU.bitwise_and,
+                )
+            else:
+                nc.scalar.activation(out=q[:, 1, :], in_=q[:, 0, :], func=ACT.Abs)
+
+        def quantise(u, g):
+            nc.vector.quantize_mx(
+                out=codes[u][:, g, :, :].rearrange("p a c -> p (a c)").bitcast(FP8X4),
+                scales=scales[u][:, g, :, :].rearrange("p a c -> p (a c)"),
+                in_=qtiles[(u, g)][:].rearrange("p a c -> p (a c)"),
+            )
+
+        def bias_transposes(n):
+            bb = tpsum.tile([P, 4 * P], BF16, tag="t")
+            bias_bank[n] = bb
+            for j in range(4):
+                nc.tensor.transpose(bb[:, j * P : (j + 1) * P], w_raw[4 * n + j][:, K : K + 1].to_broadcast([P, P]), ident_bf[:])
+
+        def bias_relu(n):
+            nc.scalar.activation(out=bias[:, 512 * n : 512 * (n + 1)], in_=bias_bank[n][:], func=ACT.Relu)
+
+        def multiply(s, m):
+            u = ("w", s)
+            xu = ("x", m // 2)
+            part_cols = slice((m % 2) * P, (m % 2 + 1) * P)
+            acc = apsum.tile([P, STEP_COLS], F32, tag="acc")
+            accs[(s, m)] = acc
+            n = 0
+            for g in range(PASSES):
+                for sg in range(2):
+                    nc.tensor.matmul_mx(
+                        out=acc[:],
+                        lhsT=codes[xu][:, g, sg, part_cols].bitcast(FP8X4),
+                        lhsT_scale=scales[xu][:, g, sg, part_cols],
+                        rhs=codes[u][:, g, sg, :].bitcast(FP8X4),
+                        rhs_scale=scales[u][:, g, sg, :],
+                        start=(n == 0),
+                        stop=(n == 2 * PASSES - 1),
+                    )
+                    n += 1
+
+        def epilogue(s, m):
+            cols = slice(STEP_COLS * s, STEP_COLS * (s + 1))
+            nc.vector.scalar_tensor_tensor(
+                out=o0[m][:, cols], in0=accs[(s, m)][:], scalar=0.5, in1=bias[:, cols], op0=ALU.mult, op1=ALU.add
+            )
+            nc.vector.tensor_reduce(
+                out=stats[:, 4 * s + m : 4 * s + m + 1],
+                in_=o0[m][:, cols],
+                axis=AX.X,
+                op=ALU.max,
+                apply_absolute_value=True,
+            )
+            if s % 2 == 1:
+                wide = slice(STEP_COLS * (s - 1), STEP_COLS * (s + 1))
+                nc.sync.dma_start(out=out_0[m * P : (m + 1) * P, wide], in_=o0[m][:, wide])
+
+        def group(s, m):
+            multiply(s, m)
+            epilogue(s, m)
+
+        G = range(PASSES)
+        X0 = ("x", 0)
+        X1 = ("x", 1)
+        W0 = ("w", 0)
+        W1 = ("w", 1)
+        W2 = ("w", 2)
+
+        transposes(X0, True, "t")
+        for g in G:
+            copy_out(X0, g, "s")
+        transposes(W0, True, "a")
+        for g in G:
+            absolute(X0, g, "v")
+        for g in G:
+            copy_out(W0, g, "s")
+        for g in G:
+            quantise(X0, g)
+        transposes(X1, True, "t")
+        for g in G:
+            absolute(W0, g, "v")
+        for g in G:
+            copy_out(X1, g, "s")
+        for g in G:
+            quantise(W0, g)
+        transposes(W1, True, "a")
+        for g in G:
+            absolute(X1, g, "v")
+        for g in G:
+            copy_out(W1, g, "s")
+        bias_transposes(0)
+        bias_relu(0)
+        for g in G:
+            quantise(X1, g)
+        group(0, 0)
+        group(0, 1)
+        for g in (1, 3):
+            absolute(W1, g, "v")
+        for g in (0, 2):
+            absolute(W1, g, "s")
+        transposes(W2, False, "t")
+        for g in G:
+            copy_out(W2, g, "s")
+        bias_transposes(1)
+        bias_relu(1)
+        for g in (1, 3, 0, 2):
+            quantise(W1, g)
+        group(0, 2)
+        group(0, 3)
+
+        q_order = (1, 3, 0, 2)
+        for s in range(1, STEPS):
+            nxt = ("w", s + 1)
+            more = s + 1 < STEPS
+            if more:
+                for g in (1, 3):
+                    absolute(nxt, g, "v")
+                for g in (0, 2):
+                    absolute(nxt, g, "s")
+            if s == STEPS - 2:
+                for g in q_order:
+                    quantise(nxt, g)
+            for m in range(4):
+                group(s, m)
+                if more and s != STEPS - 2:
+                    quantise(nxt, q_order[m])
+            if s + 2 < STEPS:
+                u = ("w", s + 2)
+                transposes(u, False, "t")
+                for g in G:
+                    copy_out(u, g, "s")
+                if (s + 2) % 2 == 0:
+                    bias_transposes((s + 2) // 2)
+                    bias_relu((s + 2) // 2)
+
+        part = const.tile([P, 1], F32, name="part")
+        nc.vector.tensor_reduce(out=part[:], in_=stats[:], axis=AX.X, op=ALU.max)
+        spread = tpsum.tile([P, P], F32, tag="t")
+        nc.tensor.transpose(spread[:], part[:, 0:1].to_broadcast([P, P]), ident[:])
+        junk = const.tile([P, P], F32, name="junk")
+        scale = const.tile([P, 1], F32, name="scale")
+        nc.vector.tensor_scalar(
+            out=junk[:], in0=spread[:], scalar1=1.0 / 448.0, scalar2=None, op0=ALU.mult, op1=ALU.max, accum_out=scale[:]
+        )
+        factor = const.tile([P, 1], F32, name="factor")
+        nc.vector.reciprocal(out=factor[:], in_=scale[:])
+
+        split = 1344
+        for m in range(4):
+            f8 = const.tile([P, OUT], FP8, name="f8_%d" % m)
+            nc.vector.tensor_scalar(
+                out=f8[:, 0:split], in0=o0[m][:, 0:split], scalar1=factor[:, 0:1], scalar2=None, op0=ALU.mult, saturate=False
+            )
+            nc.scalar.activation(
+                out=f8[:, split:OUT],
+                in_=o0[m][:, split:OUT],
+                func=ACT.Identity,
+                scale=factor[:, 0:1],
+                bias=zeros[:, 0:1],
+                saturate=False,
+            )
+            nc.sync.dma_start(out=out_1[m * P : (m + 1) * P, :], in_=f8[:].bitcast(U8))

@@ -71,11 +71,13 @@ def tile_skanlinear_kernel(tc, x, weight, out_0, out_1):
         xc = const.tile([P, 2, PASSES, 2, STEP_COLS], I32, name="xc", align_bytes=64)
         xs = const.tile([P, 2, PASSES, 2, STEP_COLS], U8, name="xs", align_bytes=64)
         bias = const.tile([P, OUT], F32, name="bias")
-        stats = const.tile([P, 4 * STEPS], F32, name="stats")
+        N_STATS = 4 * STEPS - 1
+        stats = const.tile([P, N_STATS], F32, name="stats")
         o0 = []
         for m in range(4):
-            t = const.tile([P, OUT], F32, name="o0_%d" % m)
+            t = const.tile([P, OUT + 8], F32, name="o0_%d" % m)
             o0.append(t)
+        part = const.tile([P, 1], F32, name="part")
 
         banks = {}
         qtiles = {}
@@ -143,11 +145,17 @@ def tile_skanlinear_kernel(tc, x, weight, out_0, out_1):
                 in_=qtiles[(u, g)][:].rearrange("p a c -> p (a c)"),
             )
 
-        def bias_transposes(n):
-            bb = tpsum.tile([P, 4 * P], BF16, tag="t")
+        def bias_spread(n):
+            bb = tpsum.tile([P, 4 * P], F32, tag="t")
             bias_bank[n] = bb
             for j in range(4):
-                nc.tensor.transpose(bb[:, j * P : (j + 1) * P], w_raw[4 * n + j][:, K : K + 1].to_broadcast([P, P]), ident_bf[:])
+                nc.tensor.matmul(
+                    out=bb[:, j * P : (j + 1) * P],
+                    lhsT=w_raw[4 * n + j][:, K : K + 1].to_broadcast([P, P]),
+                    rhs=ident_bf[:],
+                    start=True,
+                    stop=True,
+                )
 
         def bias_relu(n):
             nc.scalar.activation(out=bias[:, 512 * n : 512 * (n + 1)], in_=bias_bank[n][:], func=ACT.Relu)
@@ -156,7 +164,10 @@ def tile_skanlinear_kernel(tc, x, weight, out_0, out_1):
             u = ("w", s)
             xu = ("x", m // 2)
             part_cols = slice((m % 2) * P, (m % 2 + 1) * P)
-            acc = apsum.tile([P, STEP_COLS], F32, tag="acc")
+            if s == STEPS - 1:
+                acc = tpsum.tile([P, STEP_COLS], F32, tag="t")
+            else:
+                acc = apsum.tile([P, STEP_COLS], F32, tag="acc")
             accs[(s, m)] = acc
             n = 0
             for g in range(PASSES):
@@ -172,36 +183,57 @@ def tile_skanlinear_kernel(tc, x, weight, out_0, out_1):
                     )
                     n += 1
 
-        def epilogue(s, m):
+        pending = []
+        reduced = [0]
+
+        def abs_max(dst, src):
+            nc.vector.tensor_reduce(out=dst, in_=src, axis=AX.X, op=ALU.max, apply_absolute_value=True)
+
+        def reduce_pending(keep):
+            while len(pending) - reduced[0] > keep:
+                s, m = pending[reduced[0]]
+                reduced[0] += 1
+                abs_max(stats[:, 4 * s + m : 4 * s + m + 1], o0[m][:, STEP_COLS * s : STEP_COLS * (s + 1)])
+
+        def group(s, m):
+            multiply(s, m)
             cols = slice(STEP_COLS * s, STEP_COLS * (s + 1))
+            last = s == STEPS - 1 and m == 3
+            if last:
+                reduce_pending(0)
+                nc.vector.tensor_reduce(out=o0[3][:, OUT : OUT + 1], in_=stats[:], axis=AX.X, op=ALU.max)
             nc.vector.scalar_tensor_tensor(
                 out=o0[m][:, cols], in0=accs[(s, m)][:], scalar=0.5, in1=bias[:, cols], op0=ALU.mult, op1=ALU.add
             )
-            nc.vector.tensor_reduce(
-                out=stats[:, 4 * s + m : 4 * s + m + 1],
-                in_=o0[m][:, cols],
-                axis=AX.X,
-                op=ALU.max,
-                apply_absolute_value=True,
-            )
+            if last:
+                abs_max(part[:], o0[3][:, STEP_COLS * s : OUT + 1])
+            else:
+                pending.append((s, m))
             if s % 2 == 1:
                 wide = slice(STEP_COLS * (s - 1), STEP_COLS * (s + 1))
                 nc.sync.dma_start(out=out_0[m * P : (m + 1) * P, wide], in_=o0[m][:, wide])
 
-        def group(s, m):
-            multiply(s, m)
-            epilogue(s, m)
+        def absolutes(u):
+            for g in (1, 3):
+                absolute(u, g, "v")
+            for g in (0, 2):
+                absolute(u, g, "s")
+
+        def transposes_and_copies(u):
+            transposes(u, False, "t")
+            for g in range(PASSES):
+                copy_out(u, g, "s")
 
         G = range(PASSES)
         X0 = ("x", 0)
         X1 = ("x", 1)
         W0 = ("w", 0)
         W1 = ("w", 1)
-        W2 = ("w", 2)
+        q_order = (1, 3, 0, 2)
 
         transposes(X0, True, "t")
         for g in G:
-            copy_out(X0, g, "s")
+            copy_out(X0, g, "svsv"[g])
         transposes(W0, True, "a")
         for g in G:
             absolute(X0, g, "v")
@@ -221,54 +253,41 @@ def tile_skanlinear_kernel(tc, x, weight, out_0, out_1):
             absolute(X1, g, "v")
         for g in G:
             copy_out(W1, g, "s")
-        bias_transposes(0)
+        bias_spread(0)
         bias_relu(0)
         for g in G:
             quantise(X1, g)
         group(0, 0)
         group(0, 1)
-        for g in (1, 3):
-            absolute(W1, g, "v")
-        for g in (0, 2):
-            absolute(W1, g, "s")
-        transposes(W2, False, "t")
+        reduce_pending(1)
+        absolutes(W1)
+        transposes_and_copies(("w", 2))
+        reduce_pending(0)
         for g in G:
-            copy_out(W2, g, "s")
-        bias_transposes(1)
-        bias_relu(1)
-        for g in (1, 3, 0, 2):
             quantise(W1, g)
         group(0, 2)
         group(0, 3)
+        reduce_pending(1)
+        absolutes(("w", 2))
+        transposes_and_copies(("w", 3))
 
-        q_order = (1, 3, 0, 2)
         for s in range(1, STEPS):
-            nxt = ("w", s + 1)
-            more = s + 1 < STEPS
-            if more:
-                for g in (1, 3):
-                    absolute(nxt, g, "v")
-                for g in (0, 2):
-                    absolute(nxt, g, "s")
-            if s == STEPS - 2:
+            reduce_pending(0)
+            if s + 1 < STEPS:
                 for g in q_order:
-                    quantise(nxt, g)
+                    quantise(("w", s + 1), g)
             for m in range(4):
                 group(s, m)
-                if more and s != STEPS - 2:
-                    quantise(nxt, q_order[m])
+                reduce_pending(1)
+                if m == 1 and s % 2 == 1 and s + 1 < STEPS:
+                    bias_spread((s + 1) // 2)
+                    bias_relu((s + 1) // 2)
             if s + 2 < STEPS:
-                u = ("w", s + 2)
-                transposes(u, False, "t")
-                for g in G:
-                    copy_out(u, g, "s")
-                if (s + 2) % 2 == 0:
-                    bias_transposes((s + 2) // 2)
-                    bias_relu((s + 2) // 2)
+                absolutes(("w", s + 2))
+            if s + 3 < STEPS:
+                transposes_and_copies(("w", s + 3))
 
-        part = const.tile([P, 1], F32, name="part")
-        nc.vector.tensor_reduce(out=part[:], in_=stats[:], axis=AX.X, op=ALU.max)
-        spread = tpsum.tile([P, P], F32, tag="t")
+        spread = apsum.tile([P, P], F32, tag="acc")
         nc.tensor.transpose(spread[:], part[:, 0:1].to_broadcast([P, P]), ident[:])
         junk = const.tile([P, P], F32, name="junk")
         scale = const.tile([P, 1], F32, name="scale")

@@ -33,6 +33,7 @@ def tile_skanlinear_kernel(tc, x, weight, out_0, out_1):
         rawp = ctx.enter_context(tc.tile_pool(name="rawp", bufs=1))
         qpool = ctx.enter_context(tc.tile_pool(name="qpool", bufs=8))
         cpool = ctx.enter_context(tc.tile_pool(name="cpool", bufs=3))
+        opool = ctx.enter_context(tc.tile_pool(name="opool", bufs=4))
         tpsum = ctx.enter_context(tc.psum_pool(name="tpsum", bufs=4))
         apsum = ctx.enter_context(tc.psum_pool(name="apsum", bufs=4))
         ctx.enter_context(tc.manual_schedule())
@@ -80,6 +81,7 @@ def tile_skanlinear_kernel(tc, x, weight, out_0, out_1):
         part = const.tile([P, 1], F32, name="part")
 
         banks = {}
+        ordered = {}
         qtiles = {}
         codes = {}
         scales = {}
@@ -103,9 +105,12 @@ def tile_skanlinear_kernel(tc, x, weight, out_0, out_1):
                 order = [(g, j) for j in range(2) for g in range(PASSES)]
             pair = raw_pair(u)
             for g, j in order:
-                words = pair[j][:, 0:K].bitcast(F32)
                 for h in range(2):
-                    nc.tensor.transpose(banks[(u, g)][:, j, h, :], words[:, 256 * g + h : 256 * (g + 1) : 2], ident[:])
+                    if (u, j) in ordered:
+                        src = ordered[(u, j)][:, h, P * g : P * (g + 1)]
+                    else:
+                        src = pair[j][:, 0:K].bitcast(F32)[:, 256 * g + h : 256 * (g + 1) : 2]
+                    nc.tensor.transpose(banks[(u, g)][:, j, h, :], src, ident[:])
             if u[0] == "x":
                 codes[u] = xc[:, u[1], :, :, :]
                 scales[u] = xs[:, u[1], :, :, :]
@@ -114,6 +119,13 @@ def tile_skanlinear_kernel(tc, x, weight, out_0, out_1):
                 ws = cpool.tile([P, PASSES, 2, STEP_COLS], U8, tag="ws", align_bytes=64)
                 codes[u] = wc[:]
                 scales[u] = ws[:]
+
+        def put_in_order(u):
+            pair = raw_pair(u)
+            for j in range(2):
+                t = opool.tile([P, 2, K // 4], F32, tag="o")
+                ordered[(u, j)] = t
+                nc.scalar.copy(out=t[:], in_=pair[j][:, 0:K].bitcast(F32).rearrange("r (q h) -> r h q", h=2))
 
         def copy_out(u, g, eng):
             q = qpool.tile([P, 2, 4 * STEP_COLS], BF16, tag="q", align_bytes=64)
@@ -213,11 +225,24 @@ def tile_skanlinear_kernel(tc, x, weight, out_0, out_1):
                 wide = slice(STEP_COLS * (s - 1), STEP_COLS * (s + 1))
                 nc.sync.dma_start(out=out_0[m * P : (m + 1) * P, wide], in_=o0[m][:, wide])
 
+        def on_scalar(u):
+            if u[1] >= 3:
+                return (0,)
+            return (0, 2)
+
         def absolutes(u):
-            for g in (1, 3):
-                absolute(u, g, "v")
-            for g in (0, 2):
+            for g in range(PASSES):
+                if g not in on_scalar(u):
+                    absolute(u, g, "v")
+            for g in on_scalar(u):
                 absolute(u, g, "s")
+
+        def quantises(u):
+            for g in range(PASSES):
+                if g not in on_scalar(u):
+                    quantise(u, g)
+            for g in on_scalar(u):
+                quantise(u, g)
 
         def transposes_and_copies(u):
             transposes(u, False, "t")
@@ -229,7 +254,6 @@ def tile_skanlinear_kernel(tc, x, weight, out_0, out_1):
         X1 = ("x", 1)
         W0 = ("w", 0)
         W1 = ("w", 1)
-        q_order = (1, 3, 0, 2)
 
         transposes(X0, True, "t")
         for g in G:
@@ -274,11 +298,12 @@ def tile_skanlinear_kernel(tc, x, weight, out_0, out_1):
         for s in range(1, STEPS):
             reduce_pending(0)
             if s + 1 < STEPS:
-                for g in q_order:
-                    quantise(("w", s + 1), g)
+                quantises(("w", s + 1))
             for m in range(4):
                 group(s, m)
                 reduce_pending(1)
+                if m == 0 and s + 3 < STEPS:
+                    put_in_order(("w", s + 3))
                 if m == 1 and s % 2 == 1 and s + 1 < STEPS:
                     bias_spread((s + 1) // 2)
                     bias_relu((s + 1) // 2)

@@ -226,6 +226,8 @@ def tile_skanlinear_kernel(tc, x, weight, out_0, out_1):
                 nc.sync.dma_start(out=out_0[m * P : (m + 1) * P, wide], in_=o0[m][:, wide])
 
         def on_scalar(u):
+            if u[1] == 1:
+                return ()
             if u[1] >= 3:
                 return (0,)
             return (0, 2)
@@ -279,6 +281,7 @@ def tile_skanlinear_kernel(tc, x, weight, out_0, out_1):
             copy_out(W1, g, "s")
         bias_spread(0)
         bias_relu(0)
+        put_in_order(("w", 3))
         for g in G:
             quantise(X1, g)
         group(0, 0)

@@ -23,6 +23,16 @@ STEPS = OUT // STEP_COLS
 
 FLOPS = 2 * 2 * TOK * K * OUT
 
+PAIR_STT = True
+AND_RUN = 3
+WIDE_RED_STEPS = 6
+ORDER_FROM = 3
+Q_BUFS = 3
+W_RAW_BUFS = 12
+RED_A = 2
+RED_B = 2
+RED_C = 2
+
 
 def tile_skanlinear_kernel(tc, x, weight, out_0, out_1):
     nc = tc.nc
@@ -31,7 +41,7 @@ def tile_skanlinear_kernel(tc, x, weight, out_0, out_1):
     with ExitStack() as ctx:
         const = ctx.enter_context(tc.tile_pool(name="const", bufs=1))
         rawp = ctx.enter_context(tc.tile_pool(name="rawp", bufs=1))
-        qpool = ctx.enter_context(tc.tile_pool(name="qpool", bufs=8))
+        qpool = ctx.enter_context(tc.tile_pool(name="qpool", bufs=Q_BUFS))
         cpool = ctx.enter_context(tc.tile_pool(name="cpool", bufs=3))
         opool = ctx.enter_context(tc.tile_pool(name="opool", bufs=4))
         tpsum = ctx.enter_context(tc.psum_pool(name="tpsum", bufs=4))
@@ -47,7 +57,7 @@ def tile_skanlinear_kernel(tc, x, weight, out_0, out_1):
             x_raw[b] = t
 
         def load_w(i):
-            t = rawp.tile([P, K + 2], BF16, name="wraw%d" % i)
+            t = rawp.tile([P, K + 2], BF16, tag="wraw%d" % (i % W_RAW_BUFS))
             nc.sync.dma_start(out=t[:, 0 : K + 1], in_=weight[i * P : (i + 1) * P, :])
             w_raw[i] = t
 
@@ -57,7 +67,7 @@ def tile_skanlinear_kernel(tc, x, weight, out_0, out_1):
         load_w(1)
         load_x(2)
         load_x(3)
-        for i in range(2, 16):
+        for i in range(2, W_RAW_BUFS):
             load_w(i)
 
         ident = const.tile([P, P], F32, name="ident")
@@ -72,12 +82,9 @@ def tile_skanlinear_kernel(tc, x, weight, out_0, out_1):
         xc = const.tile([P, 2, PASSES, 2, STEP_COLS], I32, name="xc", align_bytes=64)
         xs = const.tile([P, 2, PASSES, 2, STEP_COLS], U8, name="xs", align_bytes=64)
         bias = const.tile([P, OUT], F32, name="bias")
-        N_STATS = 4 * STEPS - 1
-        stats = const.tile([P, N_STATS], F32, name="stats")
-        o0 = []
-        for m in range(4):
-            t = const.tile([P, OUT + 8], F32, name="o0_%d" % m)
-            o0.append(t)
+        stats = const.tile([P, 4 * STEPS], F32, name="stats")
+        n_stats = [0]
+        o0all = const.tile([P, 4, OUT + 8], F32, name="o0all")
         part = const.tile([P, 1], F32, name="part")
 
         banks = {}
@@ -119,6 +126,8 @@ def tile_skanlinear_kernel(tc, x, weight, out_0, out_1):
                 ws = cpool.tile([P, PASSES, 2, STEP_COLS], U8, tag="ws", align_bytes=64)
                 codes[u] = wc[:]
                 scales[u] = ws[:]
+            q = qpool.tile([P, PASSES, 2, 4 * STEP_COLS], BF16, tag="q", align_bytes=64)
+            qtiles[u] = q
 
         def put_in_order(u):
             pair = raw_pair(u)
@@ -128,34 +137,54 @@ def tile_skanlinear_kernel(tc, x, weight, out_0, out_1):
                 nc.scalar.copy(out=t[:], in_=pair[j][:, 0:K].bitcast(F32).rearrange("r (q h) -> r h q", h=2))
 
         def copy_out(u, g, eng):
-            q = qpool.tile([P, 2, 4 * STEP_COLS], BF16, tag="q", align_bytes=64)
-            qtiles[(u, g)] = q
-            dst = q[:, 0, :].bitcast(F32).rearrange("p (j r h) -> p j r h", j=2, h=2)
+            dst = qtiles[u][:, g, 0, :].bitcast(F32).rearrange("p (j r h) -> p j r h", j=2, h=2)
             src = banks[(u, g)][:].rearrange("p j h r -> p j r h")
             if eng == "v":
                 nc.vector.tensor_copy(out=dst, in_=src)
             else:
                 nc.scalar.copy(out=dst, in_=src)
 
-        def absolute(u, g, eng):
-            q = qtiles[(u, g)]
-            if eng == "v":
-                nc.vector.tensor_scalar(
-                    out=q[:, 1, :].bitcast(I32),
-                    in0=q[:, 0, :].bitcast(I32),
-                    scalar1=0x7FFF7FFF,
-                    scalar2=None,
-                    op0=ALU.bitwise_and,
-                )
-            else:
-                nc.scalar.activation(out=q[:, 1, :], in_=q[:, 0, :], func=ACT.Abs)
+        def and_range(u, sl):
+            q = qtiles[u]
+            nc.vector.tensor_scalar(
+                out=q[:, sl, 1, :].bitcast(I32),
+                in0=q[:, sl, 0, :].bitcast(I32),
+                scalar1=0x7FFF7FFF,
+                scalar2=None,
+                op0=ALU.bitwise_and,
+            )
+
+        def on_scalar(u):
+            if u[0] == "x" or u[1] == 0 or (u[1] == 1 and ORDER_FROM <= 3):
+                return ()
+            if u[1] >= 3:
+                return (0,)
+            return (0, 1)
+
+        def absolutes(u):
+            s_list = on_scalar(u)
+            first = len(s_list)
+            g = first
+            while g < PASSES:
+                n = min(AND_RUN, PASSES - g)
+                and_range(u, slice(g, g + n))
+                g += n
+            for g in s_list:
+                nc.scalar.activation(out=qtiles[u][:, g, 1, :], in_=qtiles[u][:, g, 0, :], func=ACT.Abs)
 
         def quantise(u, g):
             nc.vector.quantize_mx(
                 out=codes[u][:, g, :, :].rearrange("p a c -> p (a c)").bitcast(FP8X4),
                 scales=scales[u][:, g, :, :].rearrange("p a c -> p (a c)"),
-                in_=qtiles[(u, g)][:].rearrange("p a c -> p (a c)"),
+                in_=qtiles[u][:, g, :, :].rearrange("p a c -> p (a c)"),
             )
+
+        def quantises(u):
+            for g in range(PASSES):
+                if g not in on_scalar(u):
+                    quantise(u, g)
+            for g in on_scalar(u):
+                quantise(u, g)
 
         def bias_spread(n):
             bb = tpsum.tile([P, 4 * P], F32, tag="t")
@@ -172,20 +201,33 @@ def tile_skanlinear_kernel(tc, x, weight, out_0, out_1):
         def bias_relu(n):
             nc.scalar.activation(out=bias[:, 512 * n : 512 * (n + 1)], in_=bias_bank[n][:], func=ACT.Relu)
 
+        def paired(s, m):
+            return PAIR_STT and not (s == STEPS - 1 and m >= 2)
+
         def multiply(s, m):
             u = ("w", s)
             xu = ("x", m // 2)
             part_cols = slice((m % 2) * P, (m % 2 + 1) * P)
-            if s == STEPS - 1:
-                acc = tpsum.tile([P, STEP_COLS], F32, tag="t")
+            if paired(s, m):
+                if m % 2 == 0:
+                    if s == STEPS - 1:
+                        bank = tpsum.tile([P, 2, STEP_COLS], F32, tag="t")
+                    else:
+                        bank = apsum.tile([P, 2, STEP_COLS], F32, tag="acc")
+                    accs[(s, m // 2)] = bank
+                acc = accs[(s, m // 2)][:, m % 2, :]
             else:
-                acc = apsum.tile([P, STEP_COLS], F32, tag="acc")
-            accs[(s, m)] = acc
+                if s == STEPS - 1:
+                    t = tpsum.tile([P, STEP_COLS], F32, tag="t")
+                else:
+                    t = apsum.tile([P, STEP_COLS], F32, tag="acc")
+                accs[(s, m, "one")] = t
+                acc = t[:]
             n = 0
             for g in range(PASSES):
                 for sg in range(2):
                     nc.tensor.matmul_mx(
-                        out=acc[:],
+                        out=acc,
                         lhsT=codes[xu][:, g, sg, part_cols].bitcast(FP8X4),
                         lhsT_scale=scales[xu][:, g, sg, part_cols],
                         rhs=codes[u][:, g, sg, :].bitcast(FP8X4),
@@ -196,55 +238,60 @@ def tile_skanlinear_kernel(tc, x, weight, out_0, out_1):
                     n += 1
 
         pending = []
-        reduced = [0]
 
         def abs_max(dst, src):
             nc.vector.tensor_reduce(out=dst, in_=src, axis=AX.X, op=ALU.max, apply_absolute_value=True)
 
         def reduce_pending(keep):
-            while len(pending) - reduced[0] > keep:
-                s, m = pending[reduced[0]]
-                reduced[0] += 1
-                abs_max(stats[:, 4 * s + m : 4 * s + m + 1], o0[m][:, STEP_COLS * s : STEP_COLS * (s + 1)])
+            while len(pending) > keep:
+                m, lo, hi = pending[0]
+                pending.remove(pending[0])
+                abs_max(stats[:, n_stats[0] : n_stats[0] + 1], o0all[:, m, lo:hi])
+                n_stats[0] += 1
 
-        def group(s, m):
-            multiply(s, m)
+        def reduce_some(n):
+            reduce_pending(max(0, len(pending) - n))
+
+        def note_done(s, m):
+            if s < WIDE_RED_STEPS:
+                if s % 2 == 1:
+                    pending.append((m, STEP_COLS * (s - 1), STEP_COLS * (s + 1)))
+            else:
+                pending.append((m, STEP_COLS * s, STEP_COLS * (s + 1)))
+
+        def store(s, m):
+            if s % 2 == 1:
+                wide = slice(STEP_COLS * (s - 1), STEP_COLS * (s + 1))
+                nc.sync.dma_start(out=out_0[m * P : (m + 1) * P, wide], in_=o0all[:, m, wide])
+
+        def evac_pair(s, p):
+            cols = slice(STEP_COLS * s, STEP_COLS * (s + 1))
+            nc.vector.scalar_tensor_tensor(
+                out=o0all[:, 2 * p : 2 * p + 2, cols],
+                in0=accs[(s, p)][:],
+                scalar=0.5,
+                in1=bias[:, cols].unsqueeze(1).to_broadcast([P, 2, STEP_COLS]),
+                op0=ALU.mult,
+                op1=ALU.add,
+            )
+            for mm in (2 * p, 2 * p + 1):
+                note_done(s, mm)
+                store(s, mm)
+
+        def evac_one(s, m):
             cols = slice(STEP_COLS * s, STEP_COLS * (s + 1))
             last = s == STEPS - 1 and m == 3
             if last:
                 reduce_pending(0)
-                nc.vector.tensor_reduce(out=o0[3][:, OUT : OUT + 1], in_=stats[:], axis=AX.X, op=ALU.max)
+                nc.vector.tensor_reduce(out=o0all[:, 3, OUT : OUT + 1], in_=stats[:, 0 : n_stats[0]], axis=AX.X, op=ALU.max)
             nc.vector.scalar_tensor_tensor(
-                out=o0[m][:, cols], in0=accs[(s, m)][:], scalar=0.5, in1=bias[:, cols], op0=ALU.mult, op1=ALU.add
+                out=o0all[:, m, cols], in0=accs[(s, m, "one")][:], scalar=0.5, in1=bias[:, cols], op0=ALU.mult, op1=ALU.add
             )
             if last:
-                abs_max(part[:], o0[3][:, STEP_COLS * s : OUT + 1])
+                abs_max(part[:], o0all[:, 3, STEP_COLS * s : OUT + 1])
             else:
-                pending.append((s, m))
-            if s % 2 == 1:
-                wide = slice(STEP_COLS * (s - 1), STEP_COLS * (s + 1))
-                nc.sync.dma_start(out=out_0[m * P : (m + 1) * P, wide], in_=o0[m][:, wide])
-
-        def on_scalar(u):
-            if u[1] == 1:
-                return ()
-            if u[1] >= 3:
-                return (0,)
-            return (0, 2)
-
-        def absolutes(u):
-            for g in range(PASSES):
-                if g not in on_scalar(u):
-                    absolute(u, g, "v")
-            for g in on_scalar(u):
-                absolute(u, g, "s")
-
-        def quantises(u):
-            for g in range(PASSES):
-                if g not in on_scalar(u):
-                    quantise(u, g)
-            for g in on_scalar(u):
-                quantise(u, g)
+                note_done(s, m)
+            store(s, m)
 
         def transposes_and_copies(u):
             transposes(u, False, "t")
@@ -261,57 +308,64 @@ def tile_skanlinear_kernel(tc, x, weight, out_0, out_1):
         for g in G:
             copy_out(X0, g, "svsv"[g])
         transposes(W0, True, "a")
-        for g in G:
-            absolute(X0, g, "v")
+        absolutes(X0)
         for g in G:
             copy_out(W0, g, "s")
         for g in G:
             quantise(X0, g)
         transposes(X1, True, "t")
-        for g in G:
-            absolute(W0, g, "v")
+        absolutes(W0)
         for g in G:
             copy_out(X1, g, "s")
         for g in G:
             quantise(W0, g)
         transposes(W1, True, "a")
-        for g in G:
-            absolute(X1, g, "v")
+        absolutes(X1)
         for g in G:
             copy_out(W1, g, "s")
         bias_spread(0)
         bias_relu(0)
-        put_in_order(("w", 3))
+        if ORDER_FROM <= 3:
+            put_in_order(("w", 3))
+        for i in range(W_RAW_BUFS, 16):
+            load_w(i)
         for g in G:
             quantise(X1, g)
-        group(0, 0)
-        group(0, 1)
-        reduce_pending(1)
+        multiply(0, 0)
+        multiply(0, 1)
         absolutes(W1)
         transposes_and_copies(("w", 2))
-        reduce_pending(0)
+        evac_pair(0, 0)
         for g in G:
             quantise(W1, g)
-        group(0, 2)
-        group(0, 3)
-        reduce_pending(1)
+        multiply(0, 2)
+        multiply(0, 3)
         absolutes(("w", 2))
         transposes_and_copies(("w", 3))
 
         for s in range(1, STEPS):
-            reduce_pending(0)
             if s + 1 < STEPS:
                 quantises(("w", s + 1))
-            for m in range(4):
-                group(s, m)
-                reduce_pending(1)
-                if m == 0 and s + 3 < STEPS:
-                    put_in_order(("w", s + 3))
-                if m == 1 and s % 2 == 1 and s + 1 < STEPS:
-                    bias_spread((s + 1) // 2)
-                    bias_relu((s + 1) // 2)
+            reduce_some(RED_A)
+            evac_pair(s - 1, 1)
+            multiply(s, 0)
+            if s + 3 < STEPS and s + 3 >= ORDER_FROM:
+                put_in_order(("w", s + 3))
+            multiply(s, 1)
+            if s % 2 == 1 and s + 1 < STEPS:
+                bias_spread((s + 1) // 2)
+                bias_relu((s + 1) // 2)
             if s + 2 < STEPS:
                 absolutes(("w", s + 2))
+            reduce_some(RED_B)
+            evac_pair(s, 0)
+            multiply(s, 2)
+            if s == STEPS - 1:
+                reduce_some(RED_C)
+                evac_one(s, 2)
+            multiply(s, 3)
+            if s == STEPS - 1:
+                evac_one(s, 3)
             if s + 3 < STEPS:
                 transposes_and_copies(("w", s + 3))
 
@@ -329,11 +383,11 @@ def tile_skanlinear_kernel(tc, x, weight, out_0, out_1):
         for m in range(4):
             f8 = const.tile([P, OUT], FP8, name="f8_%d" % m)
             nc.vector.tensor_scalar(
-                out=f8[:, 0:split], in0=o0[m][:, 0:split], scalar1=factor[:, 0:1], scalar2=None, op0=ALU.mult, saturate=False
+                out=f8[:, 0:split], in0=o0all[:, m, 0:split], scalar1=factor[:, 0:1], scalar2=None, op0=ALU.mult, saturate=False
             )
             nc.scalar.activation(
                 out=f8[:, split:OUT],
-                in_=o0[m][:, split:OUT],
+                in_=o0all[:, m, split:OUT],
                 func=ACT.Identity,
                 scale=factor[:, 0:1],
                 bias=zeros[:, 0:1],

@@ -157,9 +157,9 @@ def tile_skanlinear_kernel(tc, x, weight, out_0, out_1):
         def on_scalar(u):
             if u[0] == "x" or u[1] == 0 or (u[1] == 1 and ORDER_FROM <= 3):
                 return ()
-            if u[1] >= 3:
+            if u[1] >= 5:
                 return (0,)
-            return (0, 1)
+            return ()
 
         def absolutes(u):
             s_list = on_scalar(u)
@@ -202,7 +202,7 @@ def tile_skanlinear_kernel(tc, x, weight, out_0, out_1):
             nc.scalar.activation(out=bias[:, 512 * n : 512 * (n + 1)], in_=bias_bank[n][:], func=ACT.Relu)
 
         def paired(s, m):
-            return PAIR_STT and not (s == STEPS - 1 and m >= 2)
+            return PAIR_STT and s < STEPS - 1
 
         def multiply(s, m):
             u = ("w", s)
@@ -238,19 +238,30 @@ def tile_skanlinear_kernel(tc, x, weight, out_0, out_1):
                     n += 1
 
         pending = []
+        fresh = [0]
 
         def abs_max(dst, src):
             nc.vector.tensor_reduce(out=dst, in_=src, axis=AX.X, op=ALU.max, apply_absolute_value=True)
+
+        n_pad = [1]
 
         def reduce_pending(keep):
             while len(pending) > keep:
                 m, lo, hi = pending[0]
                 pending.remove(pending[0])
-                abs_max(stats[:, n_stats[0] : n_stats[0] + 1], o0all[:, m, lo:hi])
-                n_stats[0] += 1
+                if lo >= STEP_COLS * (STEPS - 1):
+                    abs_max(o0all[:, 3, OUT + n_pad[0] : OUT + n_pad[0] + 1], o0all[:, m, lo:hi])
+                    n_pad[0] += 1
+                else:
+                    abs_max(stats[:, n_stats[0] : n_stats[0] + 1], o0all[:, m, lo:hi])
+                    n_stats[0] += 1
+
+        def fold_stats():
+            assert all(p[1] >= STEP_COLS * (STEPS - 1) for p in pending)
+            nc.vector.tensor_reduce(out=o0all[:, 3, OUT : OUT + 1], in_=stats[:, 0 : n_stats[0]], axis=AX.X, op=ALU.max)
 
         def reduce_some(n):
-            reduce_pending(max(0, len(pending) - n))
+            reduce_pending(max(fresh[0], len(pending) - n))
 
         def note_done(s, m):
             if s < WIDE_RED_STEPS:
@@ -274,23 +285,23 @@ def tile_skanlinear_kernel(tc, x, weight, out_0, out_1):
                 op0=ALU.mult,
                 op1=ALU.add,
             )
+            before = len(pending)
             for mm in (2 * p, 2 * p + 1):
                 note_done(s, mm)
                 store(s, mm)
+            fresh[0] = len(pending) - before
 
         def evac_one(s, m):
             cols = slice(STEP_COLS * s, STEP_COLS * (s + 1))
             last = s == STEPS - 1 and m == 3
-            if last:
-                reduce_pending(0)
-                nc.vector.tensor_reduce(out=o0all[:, 3, OUT : OUT + 1], in_=stats[:, 0 : n_stats[0]], axis=AX.X, op=ALU.max)
             nc.vector.scalar_tensor_tensor(
                 out=o0all[:, m, cols], in0=accs[(s, m, "one")][:], scalar=0.5, in1=bias[:, cols], op0=ALU.mult, op1=ALU.add
             )
             if last:
-                abs_max(part[:], o0all[:, 3, STEP_COLS * s : OUT + 1])
+                abs_max(part[:], o0all[:, 3, STEP_COLS * s : OUT + 4])
             else:
                 note_done(s, m)
+                fresh[0] = 1
             store(s, m)
 
         def transposes_and_copies(u):
@@ -343,16 +354,18 @@ def tile_skanlinear_kernel(tc, x, weight, out_0, out_1):
         absolutes(("w", 2))
         transposes_and_copies(("w", 3))
 
-        for s in range(1, STEPS):
-            if s + 1 < STEPS:
-                quantises(("w", s + 1))
+        for s in range(1, STEPS - 1):
+            if s == 1:
+                evac_pair(0, 1)
+            quantises(("w", s + 1))
             reduce_some(RED_A)
-            evac_pair(s - 1, 1)
+            if s > 1:
+                evac_pair(s - 1, 1)
             multiply(s, 0)
             if s + 3 < STEPS and s + 3 >= ORDER_FROM:
                 put_in_order(("w", s + 3))
             multiply(s, 1)
-            if s % 2 == 1 and s + 1 < STEPS:
+            if s % 2 == 1:
                 bias_spread((s + 1) // 2)
                 bias_relu((s + 1) // 2)
             if s + 2 < STEPS:
@@ -360,14 +373,27 @@ def tile_skanlinear_kernel(tc, x, weight, out_0, out_1):
             reduce_some(RED_B)
             evac_pair(s, 0)
             multiply(s, 2)
-            if s == STEPS - 1:
-                reduce_some(RED_C)
-                evac_one(s, 2)
             multiply(s, 3)
-            if s == STEPS - 1:
-                evac_one(s, 3)
             if s + 3 < STEPS:
                 transposes_and_copies(("w", s + 3))
+
+        s = STEPS - 1
+        reduce_some(2)
+        evac_pair(s - 1, 1)
+        multiply(s, 0)
+        reduce_some(2)
+        evac_one(s, 0)
+        multiply(s, 1)
+        reduce_some(2)
+        evac_one(s, 1)
+        fold_stats()
+        multiply(s, 2)
+        reduce_some(1)
+        evac_one(s, 2)
+        multiply(s, 3)
+        reduce_some(1)
+        reduce_pending(0)
+        evac_one(s, 3)
 
         spread = apsum.tile([P, P], F32, tag="acc")
         nc.tensor.transpose(spread[:], part[:, 0:1].to_broadcast([P, P]), ident[:])

@@ -405,7 +405,7 @@ def tile_skanlinear_kernel(tc, x, weight, out_0, out_1):
         factor = const.tile([P, 1], F32, name="factor")
         nc.vector.reciprocal(out=factor[:], in_=scale[:])
 
-        split = 1344
+        split = 1376
         for m in range(4):
             f8 = const.tile([P, OUT], FP8, name="f8_%d" % m)
             nc.vector.tensor_scalar(

@@ -76,6 +76,8 @@ def tile_skanlinear_kernel(tc, x, weight, out_0, out_1):
         make_identity(nc, ident_bf[:])
         zeros = const.tile([P, 1], F32, name="zeros")
         nc.vector.memset(zeros[:], 0.0)
+        idle_in = const.tile([P, 4 * P], BF16, name="idle_in")
+        nc.vector.memset(idle_in[:], 0.0)
         warm = const.tile([P, 1], F32, name="warm")
         nc.scalar.activation(out=warm[:], in_=zeros[:], func=ACT.Abs)
 
@@ -100,6 +102,9 @@ def tile_skanlinear_kernel(tc, x, weight, out_0, out_1):
                 return [x_raw[2 * u[1]], x_raw[2 * u[1] + 1]]
             return [w_raw[2 * u[1]], w_raw[2 * u[1] + 1]]
 
+        def keep_busy(region):
+            nc.tensor.matmul(out=region, lhsT=idle_in[:, 0:P], rhs=idle_in[:, 0 : region.shape[1]], start=True, stop=True)
+
         def transposes(u, by_tile, pool):
             for g in range(PASSES):
                 if pool == "t":
@@ -111,7 +116,12 @@ def tile_skanlinear_kernel(tc, x, weight, out_0, out_1):
             if by_tile:
                 order = [(g, j) for j in range(2) for g in range(PASSES)]
             pair = raw_pair(u)
+            if u == ("x", 0):
+                for g in range(PASSES):
+                    keep_busy(banks[(u, g)][:].rearrange("p j h r -> p (j h r)"))
             for g, j in order:
+                if by_tile and g == 0:
+                    keep_busy(banks[(u, g)][:, j, :, :].rearrange("p h r -> p (h r)"))
                 for h in range(2):
                     if (u, j) in ordered:
                         src = ordered[(u, j)][:, h, P * g : P * (g + 1)]

from contextlib import ExitStack

import concourse.mybir as mybir
from concourse.masks import make_identity

F32 = mybir.dt.float32
BF16 = mybir.dt.bfloat16
I32 = mybir.dt.int32
U8 = mybir.dt.uint8
FP8X4 = mybir.dt.float8_e4m3fn_x4
FP8 = mybir.dt.float8_e4m3fn
ALU = mybir.AluOpType
ACT = mybir.ActivationFunctionType
AX = mybir.AxisListType

P = 128
K = 2048
TOK = 512
OUT = 2048
PASSES = 4
STEP_COLS = 256
STEPS = OUT // STEP_COLS

FLOPS = 2 * 2 * TOK * K * OUT

PAIR_STT = True
AND_RUN = 3
WIDE_RED_STEPS = 6
ORDER_FROM = 3
Q_BUFS = 3
W_RAW_BUFS = 12
RED_A = 2
RED_B = 2
RED_C = 2


def tile_skanlinear_kernel(tc, x, weight, out_0, out_1):
    nc = tc.nc
    x2 = x.flatten_outer_dims()

    with ExitStack() as ctx:
        const = ctx.enter_context(tc.tile_pool(name="const", bufs=1))
        rawp = ctx.enter_context(tc.tile_pool(name="rawp", bufs=1))
        qpool = ctx.enter_context(tc.tile_pool(name="qpool", bufs=Q_BUFS))
        cpool = ctx.enter_context(tc.tile_pool(name="cpool", bufs=3))
        opool = ctx.enter_context(tc.tile_pool(name="opool", bufs=4))
        tpsum = ctx.enter_context(tc.psum_pool(name="tpsum", bufs=4))
        apsum = ctx.enter_context(tc.psum_pool(name="apsum", bufs=4))
        ctx.enter_context(tc.manual_schedule())

        x_raw = {}
        w_raw = {}

        def load_x(b):
            t = rawp.tile([P, K], BF16, name="xraw%d" % b)
            nc.sync.dma_start(out=t[:], in_=x2[b * P : (b + 1) * P, :])
            x_raw[b] = t

        def load_w(i):
            t = rawp.tile([P, K + 2], BF16, tag="wraw%d" % (i % W_RAW_BUFS))
            nc.sync.dma_start(out=t[:, 0 : K + 1], in_=weight[i * P : (i + 1) * P, :])
            w_raw[i] = t

        load_x(0)
        load_x(1)
        load_w(0)
        load_w(1)
        load_x(2)
        load_x(3)
        for i in range(2, W_RAW_BUFS):
            load_w(i)

        ident = const.tile([P, P], F32, name="ident")
        make_identity(nc, ident[:])
        ident_bf = const.tile([P, P], BF16, name="ident_bf")
        make_identity(nc, ident_bf[:])
        zeros = const.tile([P, 1], F32, name="zeros")
        nc.vector.memset(zeros[:], 0.0)
        idle_in = const.tile([P, 4 * P], BF16, name="idle_in")
        nc.vector.memset(idle_in[:], 0.0)
        warm = const.tile([P, 1], F32, name="warm")
        nc.scalar.activation(out=warm[:], in_=zeros[:], func=ACT.Abs)

        xc = const.tile([P, 2, PASSES, 2, STEP_COLS], I32, name="xc", align_bytes=64)
        xs = const.tile([P, 2, PASSES, 2, STEP_COLS], U8, name="xs", align_bytes=64)
        bias = const.tile([P, OUT], F32, name="bias")
        stats = const.tile([P, 4 * STEPS], F32, name="stats")
        n_stats = [0]
        o0all = const.tile([P, 4, OUT + 8], F32, name="o0all")
        part = const.tile([P, 1], F32, name="part")

        banks = {}
        ordered = {}
        qtiles = {}
        codes = {}
        scales = {}
        bias_bank = {}
        accs = {}

        def raw_pair(u):
            if u[0] == "x":
                return [x_raw[2 * u[1]], x_raw[2 * u[1] + 1]]
            return [w_raw[2 * u[1]], w_raw[2 * u[1] + 1]]

        def keep_busy(region):
            nc.tensor.matmul(out=region, lhsT=idle_in[:, 0:P], rhs=idle_in[:, 0 : region.shape[1]], start=True, stop=True)

        def transposes(u, by_tile, pool):
            for g in range(PASSES):
                if pool == "t":
                    bank = tpsum.tile([P, 2, 2, P], F32, tag="t")
                else:
                    bank = apsum.tile([P, 2, 2, P], F32, tag="acc")
                banks[(u, g)] = bank
            order = [(g, j) for g in range(PASSES) for j in range(2)]
            if by_tile:
                order = [(g, j) for j in range(2) for g in range(PASSES)]
            pair = raw_pair(u)
            if u == ("x", 0):
                for g in range(PASSES):
                    keep_busy(banks[(u, g)][:].rearrange("p j h r -> p (j h r)"))
            for g, j in order:
                if by_tile and g == 0:
                    keep_busy(banks[(u, g)][:, j, :, :].rearrange("p h r -> p (h r)"))
                for h in range(2):
                    if (u, j) in ordered:
                        src = ordered[(u, j)][:, h, P * g : P * (g + 1)]
                    else:
                        src = pair[j][:, 0:K].bitcast(F32)[:, 256 * g + h : 256 * (g + 1) : 2]
                    nc.tensor.transpose(banks[(u, g)][:, j, h, :], src, ident[:])
            if u[0] == "x":
                codes[u] = xc[:, u[1], :, :, :]
                scales[u] = xs[:, u[1], :, :, :]
            else:
                wc = cpool.tile([P, PASSES, 2, STEP_COLS], I32, tag="wc", align_bytes=64)
                ws = cpool.tile([P, PASSES, 2, STEP_COLS], U8, tag="ws", align_bytes=64)
                codes[u] = wc[:]
                scales[u] = ws[:]
            q = qpool.tile([P, PASSES, 2, 4 * STEP_COLS], BF16, tag="q", align_bytes=64)
            qtiles[u] = q

        def put_in_order(u):
            pair = raw_pair(u)
            for j in range(2):
                t = opool.tile([P, 2, K // 4], F32, tag="o")
                ordered[(u, j)] = t
                nc.scalar.copy(out=t[:], in_=pair[j][:, 0:K].bitcast(F32).rearrange("r (q h) -> r h q", h=2))

        def copy_out(u, g, eng):
            dst = qtiles[u][:, g, 0, :].bitcast(F32).rearrange("p (j r h) -> p j r h", j=2, h=2)
            src = banks[(u, g)][:].rearrange("p j h r -> p j r h")
            if eng == "v":
                nc.vector.tensor_copy(out=dst, in_=src)
            else:
                nc.scalar.copy(out=dst, in_=src)

        def and_range(u, sl):
            q = qtiles[u]
            nc.vector.tensor_scalar(
                out=q[:, sl, 1, :].bitcast(I32),
                in0=q[:, sl, 0, :].bitcast(I32),
                scalar1=0x7FFF7FFF,
                scalar2=None,
                op0=ALU.bitwise_and,
            )

        def on_scalar(u):
            if u[0] == "x" or u[1] == 0 or (u[1] == 1 and ORDER_FROM <= 3):
                return ()
            if u[1] >= 5:
                return (0,)
            return ()

        def absolutes(u):
            s_list = on_scalar(u)
            first = len(s_list)
            g = first
            while g < PASSES:
                n = min(AND_RUN, PASSES - g)
                and_range(u, slice(g, g + n))
                g += n
            for g in s_list:
                nc.scalar.activation(out=qtiles[u][:, g, 1, :], in_=qtiles[u][:, g, 0, :], func=ACT.Abs)

        def quantise(u, g):
            nc.vector.quantize_mx(
                out=codes[u][:, g, :, :].rearrange("p a c -> p (a c)").bitcast(FP8X4),
                scales=scales[u][:, g, :, :].rearrange("p a c -> p (a c)"),
                in_=qtiles[u][:, g, :, :].rearrange("p a c -> p (a c)"),
            )

        def quantises(u):
            for g in range(PASSES):
                if g not in on_scalar(u):
                    quantise(u, g)
            for g in on_scalar(u):
                quantise(u, g)

        def bias_spread(n):
            bb = tpsum.tile([P, 4 * P], F32, tag="t")
            bias_bank[n] = bb
            for j in range(4):
                nc.tensor.matmul(
                    out=bb[:, j * P : (j + 1) * P],
                    lhsT=w_raw[4 * n + j][:, K : K + 1].to_broadcast([P, P]),
                    rhs=ident_bf[:],
                    start=True,
                    stop=True,
                )

        def bias_relu(n):
            nc.scalar.activation(out=bias[:, 512 * n : 512 * (n + 1)], in_=bias_bank[n][:], func=ACT.Relu)

        def paired(s, m):
            return PAIR_STT and s < STEPS - 1

        def multiply(s, m):
            u = ("w", s)
            xu = ("x", m // 2)
            part_cols = slice((m % 2) * P, (m % 2 + 1) * P)
            if paired(s, m):
                if m % 2 == 0:
                    if s == STEPS - 1:
                        bank = tpsum.tile([P, 2, STEP_COLS], F32, tag="t")
                    else:
                        bank = apsum.tile([P, 2, STEP_COLS], F32, tag="acc")
                    accs[(s, m // 2)] = bank
                acc = accs[(s, m // 2)][:, m % 2, :]
            else:
                if s == STEPS - 1:
                    t = tpsum.tile([P, STEP_COLS], F32, tag="t")
                else:
                    t = apsum.tile([P, STEP_COLS], F32, tag="acc")
                accs[(s, m, "one")] = t
                acc = t[:]
            n = 0
            for g in range(PASSES):
                for sg in range(2):
                    nc.tensor.matmul_mx(
                        out=acc,
                        lhsT=codes[xu][:, g, sg, part_cols].bitcast(FP8X4),
                        lhsT_scale=scales[xu][:, g, sg, part_cols],
                        rhs=codes[u][:, g, sg, :].bitcast(FP8X4),
                        rhs_scale=scales[u][:, g, sg, :],
                        start=(n == 0),
                        stop=(n == 2 * PASSES - 1),
                    )
                    n += 1

        pending = []
        fresh = [0]

        def abs_max(dst, src):
            nc.vector.tensor_reduce(out=dst, in_=src, axis=AX.X, op=ALU.max, apply_absolute_value=True)

        n_pad = [1]

        def reduce_pending(keep):
            while len(pending) > keep:
                m, lo, hi = pending[0]
                pending.remove(pending[0])
                if lo >= STEP_COLS * (STEPS - 1):
                    abs_max(o0all[:, 3, OUT + n_pad[0] : OUT + n_pad[0] + 1], o0all[:, m, lo:hi])
                    n_pad[0] += 1
                else:
                    abs_max(stats[:, n_stats[0] : n_stats[0] + 1], o0all[:, m, lo:hi])
                    n_stats[0] += 1

        def fold_stats():
            assert all(p[1] >= STEP_COLS * (STEPS - 1) for p in pending)
            nc.vector.tensor_reduce(out=o0all[:, 3, OUT : OUT + 1], in_=stats[:, 0 : n_stats[0]], axis=AX.X, op=ALU.max)

        def reduce_some(n):
            reduce_pending(max(fresh[0], len(pending) - n))

        def note_done(s, m):
            if s < WIDE_RED_STEPS:
                if s % 2 == 1:
                    pending.append((m, STEP_COLS * (s - 1), STEP_COLS * (s + 1)))
            else:
                pending.append((m, STEP_COLS * s, STEP_COLS * (s + 1)))

        def store(s, m):
            if s % 2 == 1:
                wide = slice(STEP_COLS * (s - 1), STEP_COLS * (s + 1))
                nc.sync.dma_start(out=out_0[m * P : (m + 1) * P, wide], in_=o0all[:, m, wide])

        def evac_pair(s, p):
            cols = slice(STEP_COLS * s, STEP_COLS * (s + 1))
            nc.vector.scalar_tensor_tensor(
                out=o0all[:, 2 * p : 2 * p + 2, cols],
                in0=accs[(s, p)][:],
                scalar=0.5,
                in1=bias[:, cols].unsqueeze(1).to_broadcast([P, 2, STEP_COLS]),
                op0=ALU.mult,
                op1=ALU.add,
            )
            before = len(pending)
            for mm in (2 * p, 2 * p + 1):
                note_done(s, mm)
                store(s, mm)
            fresh[0] = len(pending) - before

        def evac_one(s, m):
            cols = slice(STEP_COLS * s, STEP_COLS * (s + 1))
            last = s == STEPS - 1 and m == 3
            nc.vector.scalar_tensor_tensor(
                out=o0all[:, m, cols], in0=accs[(s, m, "one")][:], scalar=0.5, in1=bias[:, cols], op0=ALU.mult, op1=ALU.add
            )
            if last:
                abs_max(part[:], o0all[:, 3, STEP_COLS * s : OUT + 4])
            else:
                note_done(s, m)
                fresh[0] = 1
            store(s, m)

        def transposes_and_copies(u):
            transposes(u, False, "t")
            for g in range(PASSES):
                copy_out(u, g, "s")

        G = range(PASSES)
        X0 = ("x", 0)
        X1 = ("x", 1)
        W0 = ("w", 0)
        W1 = ("w", 1)

        transposes(X0, True, "t")
        for g in G:
            copy_out(X0, g, "svsv"[g])
        transposes(W0, True, "a")
        absolutes(X0)
        for g in G:
            copy_out(W0, g, "s")
        for g in G:
            quantise(X0, g)
        transposes(X1, True, "t")
        absolutes(W0)
        for g in G:
            copy_out(X1, g, "s")
        for g in G:
            quantise(W0, g)
        transposes(W1, True, "a")
        absolutes(X1)
        for g in G:
            copy_out(W1, g, "s")
        bias_spread(0)
        bias_relu(0)
        if ORDER_FROM <= 3:
            put_in_order(("w", 3))
        for i in range(W_RAW_BUFS, 16):
            load_w(i)
        for g in G:
            quantise(X1, g)
        multiply(0, 0)
        multiply(0, 1)
        absolutes(W1)
        transposes_and_copies(("w", 2))
        evac_pair(0, 0)
        for g in G:
            quantise(W1, g)
        multiply(0, 2)
        multiply(0, 3)
        absolutes(("w", 2))
        transposes_and_copies(("w", 3))

        for s in range(1, STEPS - 1):
            if s == 1:
                evac_pair(0, 1)
            quantises(("w", s + 1))
            reduce_some(RED_A)
            if s > 1:
                evac_pair(s - 1, 1)
            multiply(s, 0)
            if s + 3 < STEPS and s + 3 >= ORDER_FROM:
                put_in_order(("w", s + 3))
            multiply(s, 1)
            if s % 2 == 1:
                bias_spread((s + 1) // 2)
                bias_relu((s + 1) // 2)
            if s + 2 < STEPS:
                absolutes(("w", s + 2))
            reduce_some(RED_B)
            evac_pair(s, 0)
            multiply(s, 2)
            multiply(s, 3)
            if s + 3 < STEPS:
                transposes_and_copies(("w", s + 3))

        s = STEPS - 1
        reduce_some(2)
        evac_pair(s - 1, 1)
        multiply(s, 0)
        reduce_some(2)
        evac_one(s, 0)
        multiply(s, 1)
        reduce_some(2)
        evac_one(s, 1)
        fold_stats()
        multiply(s, 2)
        reduce_some(1)
        evac_one(s, 2)
        multiply(s, 3)
        reduce_some(1)
        reduce_pending(0)
        evac_one(s, 3)

        spread = apsum.tile([P, P], F32, tag="acc")
        nc.tensor.transpose(spread[:], part[:, 0:1].to_broadcast([P, P]), ident[:])
        junk = const.tile([P, P], F32, name="junk")
        scale = const.tile([P, 1], F32, name="scale")
        nc.vector.tensor_scalar(
            out=junk[:], in0=spread[:], scalar1=1.0 / 448.0, scalar2=None, op0=ALU.mult, op1=ALU.max, accum_out=scale[:]
        )
        factor = const.tile([P, 1], F32, name="factor")
        nc.vector.reciprocal(out=factor[:], in_=scale[:])

        split = 1376
        for m in range(4):
            f8 = const.tile([P, OUT], FP8, name="f8_%d" % m)
            nc.vector.tensor_scalar(
                out=f8[:, 0:split], in0=o0all[:, m, 0:split], scalar1=factor[:, 0:1], scalar2=None, op0=ALU.mult, saturate=False
            )
            nc.scalar.activation(
                out=f8[:, split:OUT],
                in_=o0all[:, m, split:OUT],
                func=ACT.Identity,
                scale=factor[:, 0:1],
                bias=zeros[:, 0:1],
                saturate=False,
            )
            nc.sync.dma_start(out=out_1[m * P : (m + 1) * P, :], in_=f8[:].bitcast(U8))
